import numpy as np
import ml_dtypes


def mxq(x, axis, fmt="e4m3"):
    dtype, down = {"e4m3": (ml_dtypes.float8_e4m3fn, 7), "e5m2": (ml_dtypes.float8_e5m2, 14)}[fmt]
    v = np.moveaxis(np.asarray(x, np.float32).astype(ml_dtypes.bfloat16).astype(np.float64), axis, -1)
    blocks = v.reshape(v.shape[:-1] + (-1, 32))
    amax = np.abs(blocks).max(-1, keepdims=True)
    byte = np.maximum(np.where(amax > 0, np.frexp(amax)[1] - 1 + 127, 0) - down, 1)
    scale = np.exp2(byte - 127.0)
    codes = (blocks / scale).astype(np.float32).astype(dtype).astype(np.float64)
    return np.moveaxis((codes * scale).reshape(v.shape), -1, axis)


WIDE = False


def mx_kscale(k):
    if not WIDE:
        return np.ones(k)
    levels = np.array([10, -10, 5, -5, 0])
    a = np.random.permutation(np.resize(levels, k // 512 * 4)).reshape(k // 512, 4)
    idx = np.arange(k)
    return np.exp2(a[idx // 512, idx % 128 // 32])


BF16 = ml_dtypes.bfloat16


def bf(x):
    return np.asarray(x, np.float32).astype(BF16)


def f64(x):
    return np.asarray(x).astype(np.float64)


B, S, D, E, NS, C = 2, 2048, 1024, 512, 256, 512


def softmax(z):
    e = np.exp(z - z.max(-1, keepdims=True))
    return e / e.sum(-1, keepdims=True)


def setup_inputs():
    s, t = mx_kscale(D), mx_kscale(E)
    return {"x": bf(np.random.standard_normal((B, S, D)) * s),
            "Wk": bf(np.random.standard_normal((D, E)) / np.sqrt(D) / s[:, None] * t),
            "bk": bf(np.random.standard_normal(E) * 0.2 * t),
            "Wq": bf(np.random.standard_normal((D, E)) / np.sqrt(D) / s[:, None] * t),
            "bq": bf(np.random.standard_normal(E) * 0.2 * t),
            "slot_keys": bf(np.random.standard_normal((NS, E)) / t),
            "scale": bf((2.0 + 0.2 * np.random.standard_normal(1)) / np.sqrt(E))}


def reference(x, Wk, bk, Wq, bq, slot_keys, scale):
    xq = mxq(f64(x), 2, "e4m3")
    sq = mxq(f64(slot_keys), 1, "e4m3")
    k = (xq @ mxq(f64(Wk), 0, "e4m3")) + f64(bk)
    q = (xq @ mxq(f64(Wq), 0, "e4m3")) + f64(bq)
    ww = softmax((mxq(k, 2, "e4m3") @ sq.T) * f64(scale))
    rw = softmax((mxq(q, 2, "e4m3") @ sq.T) * f64(scale))
    return ww, rw

@@ -1,0 +1,236 @@
+from contextlib import ExitStack
+
+import concourse.mybir as mybir
+from concourse.masks import make_identity
+
+F32 = mybir.dt.float32
+BF16 = mybir.dt.bfloat16
+U32 = mybir.dt.uint32
+U8 = mybir.dt.uint8
+FP8X4 = mybir.dt.float8_e4m3fn_x4
+ACT = mybir.ActivationFunctionType
+ALU = mybir.AluOpType
+
+P = 128
+PACK = 4
+K_PASS = P * PACK
+
+TOKENS = 4096
+D_MODEL = 1024
+D_KEY = 512
+SLOTS = 256
+D_PASSES = D_MODEL // K_PASS
+
+GROUP = 512
+TILES = GROUP // P
+GROUPS = TOKENS // GROUP
+SIDES = 2
+
+FLOPS = 2 * TOKENS * D_MODEL * SIDES * D_KEY + 2 * TOKENS * D_KEY * SIDES * SLOTS
+
+
+def tile_slotmemoryphasor_pa_t_kernel(
+    tc, x, Wk, bk, Wq, bq, slot_keys, scale, out_0, out_1
+):
+    nc = tc.nc
+    with ExitStack() as ctx:
+        const = ctx.enter_context(tc.tile_pool(name="const", bufs=1))
+        setup = ctx.enter_context(tc.tile_pool(name="setup", bufs=2))
+        x_pool = ctx.enter_context(tc.tile_pool(name="x_pool", bufs=1))
+        xq_pool = ctx.enter_context(tc.tile_pool(name="xq_pool", bufs=2))
+        kq_pool = ctx.enter_context(tc.tile_pool(name="kq_pool", bufs=3))
+        out_pool = ctx.enter_context(tc.tile_pool(name="out_pool", bufs=4))
+        stat_pool = ctx.enter_context(tc.tile_pool(name="stat_pool", bufs=4))
+        psum_t = ctx.enter_context(tc.psum_pool(name="psum_t", bufs=2))
+        psum_p = ctx.enter_context(tc.psum_pool(name="psum_p", bufs=4))
+        psum_s = ctx.enter_context(tc.psum_pool(name="psum_s", bufs=2))
+
+        x_groups = x.flatten_outer_dims().rearrange("(g p j) d -> g p j d", p=P, j=TILES)
+        out_groups = [
+            o.flatten_outer_dims().rearrange("(g p j) s -> g p j s", p=P, j=TILES)
+            for o in (out_0, out_1)
+        ]
+        x_sb = [
+            x_pool.tile([P, TILES, D_MODEL], BF16, name="x_sb%d" % g) for g in range(GROUPS)
+        ]
+        nc.sync.dma_start(out=x_sb[0][:], in_=x_groups[0])
+
+        w_raw = {}
+        for side, w in enumerate((Wk, Wq)):
+            w_rows = w.rearrange("(c u p e) n -> c p u e n", c=D_PASSES, u=2, p=P, e=2)
+            for c in range(D_PASSES):
+                w_raw[side, c] = setup.tile(
+                    [P, PACK, D_KEY], BF16, name="w_raw%d%d" % (side, c), bufs=1
+                )
+                nc.sync.dma_start(
+                    out=w_raw[side, c][:].rearrange("p (u e) n -> p u e n", u=2),
+                    in_=w_rows[c],
+                )
+        sk_sb = setup.tile([P, SLOTS // P, D_KEY], BF16, bufs=1)
+        nc.sync.dma_start(out=sk_sb[:], in_=slot_keys.rearrange("(h p) e -> p h e", p=P))
+        for g in range(1, GROUPS):
+            nc.sync.dma_start(out=x_sb[g][:], in_=x_groups[g])
+
+        scale_bf = const.tile([P, 1], BF16)
+        nc.scalar.dma_start(out=scale_bf[:], in_=scale.partition_broadcast(P))
+        bias = []
+        for side, b in enumerate((bk, bq)):
+            bias.append(const.tile([P, PACK], BF16, name="bias%d" % side))
+            nc.scalar.dma_start(out=bias[side][:], in_=b.rearrange("(p m) -> p m", m=PACK))
+
+        ident = const.tile([P, P], F32)
+        make_identity(nc, ident[:])
+
+        sign_scale = const.tile([P, 1], F32)
+        nc.scalar.activation(out=sign_scale[:], in_=scale_bf[:], func=ACT.Sign)
+        abs_scale = const.tile([P, 1], F32)
+        nc.scalar.activation(out=abs_scale[:], in_=scale_bf[:], func=ACT.Abs)
+        neg_abs_scale = const.tile([P, 1], F32)
+        nc.vector.tensor_scalar_mul(out=neg_abs_scale[:], in0=abs_scale[:], scalar1=-1.0)
+
+        w_codes = const.tile([P, SIDES, D_PASSES, D_KEY], U32, align_bytes=64)
+        w_scales = const.tile([P, SIDES, D_PASSES, D_KEY], U8, align_bytes=64)
+        for side in range(SIDES):
+            for c in range(D_PASSES):
+                w_grouped = setup.tile([P, D_KEY * PACK], BF16, align_bytes=64)
+                nc.vector.tensor_copy(
+                    out=w_grouped[:].rearrange("p (m r t) -> p m r t", m=PACK, t=PACK),
+                    in_=w_raw[side, c][:].rearrange("p t (r m) -> p m r t", m=PACK),
+                )
+                nc.vector.quantize_mx(
+                    out=w_codes[:, side, c, :].bitcast(FP8X4),
+                    scales=w_scales[:, side, c, :],
+                    in_=w_grouped[:],
+                )
+
+        sk_t = psum_t.tile([P, 2, SLOTS], F32, tag="xt")
+        for h in range(SLOTS // P):
+            sk_words = sk_sb[:, h, :].bitcast(F32).rearrange("p (w u) -> p u w", u=2)
+            for u in range(2):
+                nc.tensor.transpose(sk_t[:, u, h * P : (h + 1) * P], sk_words[:, u, :], ident[:])
+        sk_grouped = setup.tile([P, SLOTS * PACK], BF16, align_bytes=64, bufs=1)
+        nc.scalar.activation(
+            out=sk_grouped[:].rearrange("p (s u e) -> p s u e", u=2, e=2),
+            in_=sk_t[:].bitcast(BF16).rearrange("p u (s e) -> p s u e", e=2),
+            func=ACT.Copy,
+            scale=sign_scale[:],
+        )
+        sk_codes = const.tile([P, SLOTS], U32, align_bytes=64)
+        sk_scales = const.tile([P, SLOTS], U8, align_bytes=64)
+        nc.vector.quantize_mx(
+            out=sk_codes[:].bitcast(FP8X4), scales=sk_scales[:], in_=sk_grouped[:]
+        )
+
+        def quantise_x(g):
+            x_grouped = xq_pool.tile([P, D_PASSES, GROUP * PACK], BF16, align_bytes=64)
+            x_codes = xq_pool.tile([P, D_PASSES, GROUP], U32, align_bytes=64)
+            x_scales = xq_pool.tile([P, D_PASSES, GROUP], U8, align_bytes=64)
+            for c in range(D_PASSES):
+                for pair in range(TILES // 2):
+                    xt = psum_t.tile([P, 2, 2 * P], F32, tag="xt")
+                    for u in range(2):
+                        for i in range(2):
+                            x_words = x_sb[g][:, 2 * pair + i, :].bitcast(F32)
+                            first = (2 * c + u) * P
+                            nc.tensor.transpose(
+                                xt[:, u, i * P : (i + 1) * P],
+                                x_words[:, first : first + P],
+                                ident[:],
+                            )
+                    half = GROUP * PACK // 2
+                    nc.scalar.copy(
+                        out=x_grouped[:, c, pair * half : (pair + 1) * half]
+                        .bitcast(F32)
+                        .rearrange("p (r u) -> p r u", u=2),
+                        in_=xt[:].rearrange("p u r -> p r u"),
+                    )
+                nc.vector.quantize_mx(
+                    out=x_codes[:, c, :].bitcast(FP8X4),
+                    scales=x_scales[:, c, :],
+                    in_=x_grouped[:, c, :],
+                )
+            return x_codes, x_scales
+
+        def project(x_codes, x_scales, side):
+            kq_grouped = kq_pool.tile([P, GROUP * PACK], BF16, align_bytes=64)
+            kq_codes = kq_pool.tile([P, GROUP], U32, align_bytes=64)
+            kq_scales = kq_pool.tile([P, GROUP], U8, align_bytes=64)
+            for j in range(TILES):
+                tokens = slice(j * P, (j + 1) * P)
+                acc = psum_p.tile([P, PACK, P], F32)
+                for m in range(PACK):
+                    chunk = slice(m * P, (m + 1) * P)
+                    for c in range(D_PASSES):
+                        nc.tensor.matmul_mx(
+                            out=acc[:, m, :],
+                            lhsT=w_codes[:, side, c, chunk].bitcast(FP8X4),
+                            lhsT_scale=w_scales[:, side, c, chunk],
+                            rhs=x_codes[:, c, tokens].bitcast(FP8X4),
+                            rhs_scale=x_scales[:, c, tokens],
+                            start=(c == 0),
+                            stop=(c == D_PASSES - 1),
+                        )
+                nc.vector.tensor_tensor(
+                    out=kq_grouped[:, j * K_PASS : (j + 1) * K_PASS].rearrange(
+                        "p (r m) -> p r m", m=PACK
+                    ),
+                    in0=acc[:].rearrange("p m r -> p r m"),
+                    in1=bias[side][:].unsqueeze(1).to_broadcast([P, P, PACK]),
+                    op=ALU.add,
+                )
+            nc.vector.quantize_mx(
+                out=kq_codes[:].bitcast(FP8X4), scales=kq_scales[:], in_=kq_grouped[:]
+            )
+            return kq_codes, kq_scales
+
+        def attend(kq_codes, kq_scales, g, side):
+            probs = out_pool.tile([P, TILES, SLOTS], F32)
+            top = stat_pool.tile([P, TILES], F32)
+            shift = stat_pool.tile([P, TILES], F32)
+            total = stat_pool.tile([P, TILES], F32)
+            inverse = stat_pool.tile([P, TILES], F32)
+            for pair in range(TILES // 2):
+                two = slice(2 * pair, 2 * pair + 2)
+                sc = psum_s.tile([P, 2, SLOTS], F32)
+                for i in range(2):
+                    tokens = slice((2 * pair + i) * P, (2 * pair + i + 1) * P)
+                    nc.tensor.matmul_mx(
+                        out=sc[:, i, :],
+                        lhsT=kq_codes[:, tokens].bitcast(FP8X4),
+                        lhsT_scale=kq_scales[:, tokens],
+                        rhs=sk_codes[:].bitcast(FP8X4),
+                        rhs_scale=sk_scales[:],
+                        start=True,
+                        stop=True,
+                    )
+                nc.vector.tensor_reduce(
+                    out=top[:, two], in_=sc[:], axis=mybir.AxisListType.X, op=ALU.max
+                )
+                nc.vector.tensor_scalar_mul(
+                    out=shift[:, two], in0=top[:, two], scalar1=neg_abs_scale[:]
+                )
+                for i in range(2):
+                    j = 2 * pair + i
+                    nc.scalar.activation(
+                        out=probs[:, j, :],
+                        in_=sc[:, i, :],
+                        func=ACT.Exp,
+                        bias=shift[:, j : j + 1],
+                        scale=abs_scale[:],
+                        accum_out=total[:, j : j + 1],
+                    )
+            nc.vector.reciprocal(out=inverse[:], in_=total[:])
+            for j in range(TILES):
+                nc.scalar.activation(
+                    out=probs[:, j, :],
+                    in_=probs[:, j, :],
+                    func=ACT.Copy,
+                    scale=inverse[:, j : j + 1],
+                )
+            nc.sync.dma_start(out=out_groups[side][g], in_=probs[:])
+
+        for g in range(GROUPS):
+            x_codes, x_scales = quantise_x(g)
+            for side in range(SIDES):
+                kq_codes, kq_scales = project(x_codes, x_scales, side)
+                attend(kq_codes, kq_scales, g, side)

@@ -25,6 +25,8 @@ GROUP = 512
 TILES = GROUP // P
 GROUPS = TOKENS // GROUP
 SIDES = 2
+HALVES = GROUPS * D_PASSES
+UNITS = GROUPS * SIDES
 
 FLOPS = 2 * TOKENS * D_MODEL * SIDES * D_KEY + 2 * TOKENS * D_KEY * SIDES * SLOTS
 
@@ -34,42 +36,41 @@ def tile_slotmemoryphasor_pa_t_kernel(
 ):
     nc = tc.nc
     with ExitStack() as ctx:
+        ctx.enter_context(tc.manual_schedule())
         const = ctx.enter_context(tc.tile_pool(name="const", bufs=1))
-        setup = ctx.enter_context(tc.tile_pool(name="setup", bufs=2))
         x_pool = ctx.enter_context(tc.tile_pool(name="x_pool", bufs=1))
-        xq_pool = ctx.enter_context(tc.tile_pool(name="xq_pool", bufs=2))
-        kq_pool = ctx.enter_context(tc.tile_pool(name="kq_pool", bufs=3))
+        xg_pool = ctx.enter_context(tc.tile_pool(name="xg_pool", bufs=3))
+        xq_pool = ctx.enter_context(tc.tile_pool(name="xq_pool", bufs=4))
+        kq_pool = ctx.enter_context(tc.tile_pool(name="kq_pool", bufs=2))
         out_pool = ctx.enter_context(tc.tile_pool(name="out_pool", bufs=4))
         stat_pool = ctx.enter_context(tc.tile_pool(name="stat_pool", bufs=4))
         psum_t = ctx.enter_context(tc.psum_pool(name="psum_t", bufs=2))
         psum_p = ctx.enter_context(tc.psum_pool(name="psum_p", bufs=4))
         psum_s = ctx.enter_context(tc.psum_pool(name="psum_s", bufs=2))
 
-        x_groups = x.flatten_outer_dims().rearrange("(g p j) d -> g p j d", p=P, j=TILES)
-        out_groups = [
-            o.flatten_outer_dims().rearrange("(g p j) s -> g p j s", p=P, j=TILES)
-            for o in (out_0, out_1)
-        ]
-        x_sb = [
-            x_pool.tile([P, TILES, D_MODEL], BF16, name="x_sb%d" % g) for g in range(GROUPS)
-        ]
-        nc.sync.dma_start(out=x_sb[0][:], in_=x_groups[0])
-
         w_raw = {}
         for side, w in enumerate((Wk, Wq)):
             w_rows = w.rearrange("(c u p e) n -> c p u e n", c=D_PASSES, u=2, p=P, e=2)
             for c in range(D_PASSES):
-                w_raw[side, c] = setup.tile(
-                    [P, PACK, D_KEY], BF16, name="w_raw%d%d" % (side, c), bufs=1
-                )
+                w_raw[side, c] = const.tile([P, PACK, D_KEY], BF16, name="w_raw%d%d" % (side, c))
                 nc.sync.dma_start(
                     out=w_raw[side, c][:].rearrange("p (u e) n -> p u e n", u=2),
                     in_=w_rows[c],
                 )
-        sk_sb = setup.tile([P, SLOTS // P, D_KEY], BF16, bufs=1)
-        nc.sync.dma_start(out=sk_sb[:], in_=slot_keys.rearrange("(h p) e -> p h e", p=P))
-        for g in range(1, GROUPS):
-            nc.sync.dma_start(out=x_sb[g][:], in_=x_groups[g])
+        sk_sb = const.tile([P, SLOTS // P, D_KEY], BF16)
+        nc.sync.dma_start(out=sk_sb[:], in_=slot_keys.rearrange("(blk p) e -> p blk e", p=P))
+
+        x_halves = x.flatten_outer_dims().rearrange(
+            "(g p j) (c d) -> g c p j d", p=P, j=TILES, c=D_PASSES
+        )
+        out_groups = [
+            o.flatten_outer_dims().rearrange("(g p j) s -> g p j s", p=P, j=TILES)
+            for o in (out_0, out_1)
+        ]
+        x_sb = []
+        for h in range(HALVES):
+            x_sb.append(x_pool.tile([P, TILES, K_PASS], BF16, name="x_sb%d" % h))
+            nc.sync.dma_start(out=x_sb[h][:], in_=x_halves[h // D_PASSES, h % D_PASSES])
 
         scale_bf = const.tile([P, 1], BF16)
         nc.scalar.dma_start(out=scale_bf[:], in_=scale.partition_broadcast(P))
@@ -86,29 +87,36 @@ def tile_slotmemoryphasor_pa_t_kernel(
         abs_scale = const.tile([P, 1], F32)
         nc.scalar.activation(out=abs_scale[:], in_=scale_bf[:], func=ACT.Abs)
         neg_abs_scale = const.tile([P, 1], F32)
-        nc.vector.tensor_scalar_mul(out=neg_abs_scale[:], in0=abs_scale[:], scalar1=-1.0)
+        nc.scalar.mul(out=neg_abs_scale[:], in_=abs_scale[:], mul=-1.0)
 
         w_codes = const.tile([P, SIDES, D_PASSES, D_KEY], U32, align_bytes=64)
         w_scales = const.tile([P, SIDES, D_PASSES, D_KEY], U8, align_bytes=64)
+        w_grouped = {}
         for side in range(SIDES):
             for c in range(D_PASSES):
-                w_grouped = setup.tile([P, D_KEY * PACK], BF16, align_bytes=64)
+                w_grouped[side, c] = const.tile(
+                    [P, D_KEY * PACK], BF16, align_bytes=64, name="w_grouped%d%d" % (side, c)
+                )
                 nc.vector.tensor_copy(
-                    out=w_grouped[:].rearrange("p (m r t) -> p m r t", m=PACK, t=PACK),
+                    out=w_grouped[side, c][:].rearrange("p (m r t) -> p m r t", m=PACK, t=PACK),
                     in_=w_raw[side, c][:].rearrange("p t (r m) -> p m r t", m=PACK),
                 )
+        for side in range(SIDES):
+            for c in range(D_PASSES):
                 nc.vector.quantize_mx(
                     out=w_codes[:, side, c, :].bitcast(FP8X4),
                     scales=w_scales[:, side, c, :],
-                    in_=w_grouped[:],
+                    in_=w_grouped[side, c][:],
                 )
 
         sk_t = psum_t.tile([P, 2, SLOTS], F32, tag="xt")
-        for h in range(SLOTS // P):
-            sk_words = sk_sb[:, h, :].bitcast(F32).rearrange("p (w u) -> p u w", u=2)
+        for blk in range(SLOTS // P):
+            sk_words = sk_sb[:, blk, :].bitcast(F32).rearrange("p (w u) -> p u w", u=2)
             for u in range(2):
-                nc.tensor.transpose(sk_t[:, u, h * P : (h + 1) * P], sk_words[:, u, :], ident[:])
-        sk_grouped = setup.tile([P, SLOTS * PACK], BF16, align_bytes=64, bufs=1)
+                nc.tensor.transpose(
+                    sk_t[:, u, blk * P : (blk + 1) * P], sk_words[:, u, :], ident[:]
+                )
+        sk_grouped = const.tile([P, SLOTS * PACK], BF16, align_bytes=64)
         nc.scalar.activation(
             out=sk_grouped[:].rearrange("p (s u e) -> p s u e", u=2, e=2),
             in_=sk_t[:].bitcast(BF16).rearrange("p u (s e) -> p s u e", e=2),
@@ -121,104 +129,115 @@ def tile_slotmemoryphasor_pa_t_kernel(
             out=sk_codes[:].bitcast(FP8X4), scales=sk_scales[:], in_=sk_grouped[:]
         )
 
-        def quantise_x(g):
-            x_grouped = xq_pool.tile([P, D_PASSES, GROUP * PACK], BF16, align_bytes=64)
-            x_codes = xq_pool.tile([P, D_PASSES, GROUP], U32, align_bytes=64)
-            x_scales = xq_pool.tile([P, D_PASSES, GROUP], U8, align_bytes=64)
-            for c in range(D_PASSES):
-                for pair in range(TILES // 2):
-                    xt = psum_t.tile([P, 2, 2 * P], F32, tag="xt")
-                    for u in range(2):
-                        for i in range(2):
-                            x_words = x_sb[g][:, 2 * pair + i, :].bitcast(F32)
-                            first = (2 * c + u) * P
-                            nc.tensor.transpose(
-                                xt[:, u, i * P : (i + 1) * P],
-                                x_words[:, first : first + P],
-                                ident[:],
-                            )
-                    half = GROUP * PACK // 2
-                    nc.scalar.copy(
-                        out=x_grouped[:, c, pair * half : (pair + 1) * half]
-                        .bitcast(F32)
-                        .rearrange("p (r u) -> p r u", u=2),
-                        in_=xt[:].rearrange("p u r -> p r u"),
-                    )
-                nc.vector.quantize_mx(
-                    out=x_codes[:, c, :].bitcast(FP8X4),
-                    scales=x_scales[:, c, :],
-                    in_=x_grouped[:, c, :],
-                )
-            return x_codes, x_scales
+        x_grouped = {}
+        x_mx = {}
+        kq_grouped = {}
+        kq_mx = {}
+        soft = {}
 
-        def project(x_codes, x_scales, side):
-            kq_grouped = kq_pool.tile([P, GROUP * PACK], BF16, align_bytes=64)
-            kq_codes = kq_pool.tile([P, GROUP], U32, align_bytes=64)
-            kq_scales = kq_pool.tile([P, GROUP], U8, align_bytes=64)
+        def transpose_x(h):
+            x_grouped[h] = xg_pool.tile([P, GROUP * PACK], BF16, align_bytes=64, name="x_grouped")
+            for pair in range(TILES // 2):
+                xt = psum_t.tile([P, 2, 2 * P], F32, tag="xt")
+                for u in range(2):
+                    for i in range(2):
+                        x_words = x_sb[h][:, 2 * pair + i, :].bitcast(F32)
+                        nc.tensor.transpose(
+                            xt[:, u, i * P : (i + 1) * P], x_words[:, u * P : (u + 1) * P], ident[:]
+                        )
+                width = GROUP * PACK // 2
+                nc.scalar.copy(
+                    out=x_grouped[h][:, pair * width : (pair + 1) * width]
+                    .bitcast(F32)
+                    .rearrange("p (r u) -> p r u", u=2),
+                    in_=xt[:].rearrange("p u r -> p r u"),
+                )
+
+        def quantise_x(h):
+            codes = xq_pool.tile([P, GROUP], U32, align_bytes=64, name="x_codes")
+            scales = xq_pool.tile([P, GROUP], U8, align_bytes=64, name="x_scales")
+            nc.vector.quantize_mx(
+                out=codes[:].bitcast(FP8X4), scales=scales[:], in_=x_grouped[h][:]
+            )
+            x_mx[h] = (codes, scales)
+
+        def project(n):
+            g, side = divmod(n, SIDES)
+            kq_grouped[n] = kq_pool.tile(
+                [P, GROUP * PACK], BF16, align_bytes=64, name="kq_grouped"
+            )
             for j in range(TILES):
                 tokens = slice(j * P, (j + 1) * P)
                 acc = psum_p.tile([P, PACK, P], F32)
                 for m in range(PACK):
                     chunk = slice(m * P, (m + 1) * P)
                     for c in range(D_PASSES):
+                        codes, scales = x_mx[D_PASSES * g + c]
                         nc.tensor.matmul_mx(
                             out=acc[:, m, :],
                             lhsT=w_codes[:, side, c, chunk].bitcast(FP8X4),
                             lhsT_scale=w_scales[:, side, c, chunk],
-                            rhs=x_codes[:, c, tokens].bitcast(FP8X4),
-                            rhs_scale=x_scales[:, c, tokens],
+                            rhs=codes[:, tokens].bitcast(FP8X4),
+                            rhs_scale=scales[:, tokens],
                             start=(c == 0),
                             stop=(c == D_PASSES - 1),
                         )
                 nc.vector.tensor_tensor(
-                    out=kq_grouped[:, j * K_PASS : (j + 1) * K_PASS].rearrange(
+                    out=kq_grouped[n][:, j * K_PASS : (j + 1) * K_PASS].rearrange(
                         "p (r m) -> p r m", m=PACK
                     ),
                     in0=acc[:].rearrange("p m r -> p r m"),
                     in1=bias[side][:].unsqueeze(1).to_broadcast([P, P, PACK]),
                     op=ALU.add,
                 )
-            nc.vector.quantize_mx(
-                out=kq_codes[:].bitcast(FP8X4), scales=kq_scales[:], in_=kq_grouped[:]
-            )
-            return kq_codes, kq_scales
 
-        def attend(kq_codes, kq_scales, g, side):
+        def quantise_kq(n):
+            codes = kq_pool.tile([P, GROUP], U32, align_bytes=64, name="kq_codes")
+            scales = kq_pool.tile([P, GROUP], U8, align_bytes=64, name="kq_scales")
+            nc.vector.quantize_mx(
+                out=codes[:].bitcast(FP8X4), scales=scales[:], in_=kq_grouped[n][:]
+            )
+            kq_mx[n] = (codes, scales)
+
+        def score(n):
+            codes, scales = kq_mx[n]
             probs = out_pool.tile([P, TILES, SLOTS], F32)
-            top = stat_pool.tile([P, TILES], F32)
-            shift = stat_pool.tile([P, TILES], F32)
             total = stat_pool.tile([P, TILES], F32)
-            inverse = stat_pool.tile([P, TILES], F32)
             for pair in range(TILES // 2):
-                two = slice(2 * pair, 2 * pair + 2)
                 sc = psum_s.tile([P, 2, SLOTS], F32)
                 for i in range(2):
                     tokens = slice((2 * pair + i) * P, (2 * pair + i + 1) * P)
                     nc.tensor.matmul_mx(
                         out=sc[:, i, :],
-                        lhsT=kq_codes[:, tokens].bitcast(FP8X4),
-                        lhsT_scale=kq_scales[:, tokens],
+                        lhsT=codes[:, tokens].bitcast(FP8X4),
+                        lhsT_scale=scales[:, tokens],
                         rhs=sk_codes[:].bitcast(FP8X4),
                         rhs_scale=sk_scales[:],
                         start=True,
                         stop=True,
                     )
+                top = stat_pool.tile([P, 2], F32)
                 nc.vector.tensor_reduce(
-                    out=top[:, two], in_=sc[:], axis=mybir.AxisListType.X, op=ALU.max
+                    out=top[:], in_=sc[:], axis=mybir.AxisListType.X, op=ALU.max
                 )
-                nc.vector.tensor_scalar_mul(
-                    out=shift[:, two], in0=top[:, two], scalar1=neg_abs_scale[:]
-                )
+                shift = stat_pool.tile([P, 2], F32)
+                nc.gpsimd.tensor_scalar_mul(out=shift[:], in0=top[:], scalar1=neg_abs_scale[:])
                 for i in range(2):
                     j = 2 * pair + i
                     nc.scalar.activation(
                         out=probs[:, j, :],
                         in_=sc[:, i, :],
                         func=ACT.Exp,
-                        bias=shift[:, j : j + 1],
+                        bias=shift[:, i : i + 1],
                         scale=abs_scale[:],
                         accum_out=total[:, j : j + 1],
                     )
+            soft[n] = (probs, total)
+
+        def normalise_and_store(n):
+            g, side = divmod(n, SIDES)
+            probs, total = soft[n]
+            inverse = stat_pool.tile([P, TILES], F32)
             nc.vector.reciprocal(out=inverse[:], in_=total[:])
             for j in range(TILES):
                 nc.scalar.activation(
@@ -229,8 +248,20 @@ def tile_slotmemoryphasor_pa_t_kernel(
                 )
             nc.sync.dma_start(out=out_groups[side][g], in_=probs[:])
 
-        for g in range(GROUPS):
-            x_codes, x_scales = quantise_x(g)
-            for side in range(SIDES):
-                kq_codes, kq_scales = project(x_codes, x_scales, side)
-                attend(kq_codes, kq_scales, g, side)
+        for h in range(3):
+            transpose_x(h)
+        for h in range(2):
+            quantise_x(h)
+        for n in range(UNITS + 2):
+            if n < UNITS:
+                project(n)
+            if n >= 2:
+                normalise_and_store(n - 2)
+            if n + 2 < HALVES:
+                quantise_x(n + 2)
+            if 1 <= n <= UNITS:
+                score(n - 1)
+            if n + 3 < HALVES:
+                transpose_x(n + 3)
+            if n < UNITS:
+                quantise_kq(n)

@@ -27,6 +27,7 @@ GROUPS = TOKENS // GROUP
 SIDES = 2
 HALVES = GROUPS * D_PASSES
 UNITS = GROUPS * SIDES
+PAIRS = TILES // 2
 
 FLOPS = 2 * TOKENS * D_MODEL * SIDES * D_KEY + 2 * TOKENS * D_KEY * SIDES * SLOTS
 
@@ -42,8 +43,8 @@ def tile_slotmemoryphasor_pa_t_kernel(
         xg_pool = ctx.enter_context(tc.tile_pool(name="xg_pool", bufs=3))
         xq_pool = ctx.enter_context(tc.tile_pool(name="xq_pool", bufs=4))
         kq_pool = ctx.enter_context(tc.tile_pool(name="kq_pool", bufs=2))
-        out_pool = ctx.enter_context(tc.tile_pool(name="out_pool", bufs=4))
-        stat_pool = ctx.enter_context(tc.tile_pool(name="stat_pool", bufs=4))
+        out_pool = ctx.enter_context(tc.tile_pool(name="out_pool", bufs=8))
+        stat_pool = ctx.enter_context(tc.tile_pool(name="stat_pool", bufs=8))
         psum_t = ctx.enter_context(tc.psum_pool(name="psum_t", bufs=2))
         psum_p = ctx.enter_context(tc.psum_pool(name="psum_p", bufs=4))
         psum_s = ctx.enter_context(tc.psum_pool(name="psum_s", bufs=2))
@@ -88,6 +89,8 @@ def tile_slotmemoryphasor_pa_t_kernel(
         nc.scalar.activation(out=abs_scale[:], in_=scale_bf[:], func=ACT.Abs)
         neg_abs_scale = const.tile([P, 1], F32)
         nc.scalar.mul(out=neg_abs_scale[:], in_=abs_scale[:], mul=-1.0)
+        minus_one = const.tile([P, 2], F32)
+        nc.gpsimd.memset(minus_one[:], -1.0)
 
         w_codes = const.tile([P, SIDES, D_PASSES, D_KEY], U32, align_bytes=64)
         w_scales = const.tile([P, SIDES, D_PASSES, D_KEY], U8, align_bytes=64)
@@ -137,7 +140,7 @@ def tile_slotmemoryphasor_pa_t_kernel(
 
         def transpose_x(h):
             x_grouped[h] = xg_pool.tile([P, GROUP * PACK], BF16, align_bytes=64, name="x_grouped")
-            for pair in range(TILES // 2):
+            for pair in range(PAIRS):
                 xt = psum_t.tile([P, 2, 2 * P], F32, tag="xt")
                 for u in range(2):
                     for i in range(2):
@@ -199,54 +202,52 @@ def tile_slotmemoryphasor_pa_t_kernel(
             )
             kq_mx[n] = (codes, scales)
 
-        def score(n):
+        def score(n, pair):
             codes, scales = kq_mx[n]
-            probs = out_pool.tile([P, TILES, SLOTS], F32)
-            total = stat_pool.tile([P, TILES], F32)
-            for pair in range(TILES // 2):
-                sc = psum_s.tile([P, 2, SLOTS], F32)
-                for i in range(2):
-                    tokens = slice((2 * pair + i) * P, (2 * pair + i + 1) * P)
-                    nc.tensor.matmul_mx(
-                        out=sc[:, i, :],
-                        lhsT=codes[:, tokens].bitcast(FP8X4),
-                        lhsT_scale=scales[:, tokens],
-                        rhs=sk_codes[:].bitcast(FP8X4),
-                        rhs_scale=sk_scales[:],
-                        start=True,
-                        stop=True,
-                    )
-                top = stat_pool.tile([P, 2], F32)
-                nc.vector.tensor_reduce(
-                    out=top[:], in_=sc[:], axis=mybir.AxisListType.X, op=ALU.max
+            sc = psum_s.tile([P, 2, SLOTS], F32)
+            for i in range(2):
+                tokens = slice((2 * pair + i) * P, (2 * pair + i + 1) * P)
+                nc.tensor.matmul_mx(
+                    out=sc[:, i, :],
+                    lhsT=codes[:, tokens].bitcast(FP8X4),
+                    lhsT_scale=scales[:, tokens],
+                    rhs=sk_codes[:].bitcast(FP8X4),
+                    rhs_scale=sk_scales[:],
+                    start=True,
+                    stop=True,
                 )
-                shift = stat_pool.tile([P, 2], F32)
-                nc.gpsimd.tensor_scalar_mul(out=shift[:], in0=top[:], scalar1=neg_abs_scale[:])
-                for i in range(2):
-                    j = 2 * pair + i
-                    nc.scalar.activation(
-                        out=probs[:, j, :],
-                        in_=sc[:, i, :],
-                        func=ACT.Exp,
-                        bias=shift[:, i : i + 1],
-                        scale=abs_scale[:],
-                        accum_out=total[:, j : j + 1],
-                    )
-            soft[n] = (probs, total)
-
-        def normalise_and_store(n):
-            g, side = divmod(n, SIDES)
-            probs, total = soft[n]
-            inverse = stat_pool.tile([P, TILES], F32)
-            nc.vector.reciprocal(out=inverse[:], in_=total[:])
-            for j in range(TILES):
+            top = stat_pool.tile([P, 2], F32)
+            nc.vector.tensor_reduce(out=top[:], in_=sc[:], axis=mybir.AxisListType.X, op=ALU.max)
+            shift = stat_pool.tile([P, 2], F32)
+            nc.gpsimd.tensor_scalar_mul(out=shift[:], in0=top[:], scalar1=neg_abs_scale[:])
+            probs = out_pool.tile([P, 2, SLOTS], F32)
+            total = stat_pool.tile([P, 2], F32)
+            for i in range(2):
                 nc.scalar.activation(
-                    out=probs[:, j, :],
-                    in_=probs[:, j, :],
-                    func=ACT.Copy,
-                    scale=inverse[:, j : j + 1],
+                    out=probs[:, i, :],
+                    in_=sc[:, i, :],
+                    func=ACT.Exp,
+                    bias=shift[:, i : i + 1],
+                    scale=abs_scale[:],
+                    accum_out=total[:, i : i + 1],
                 )
-            nc.sync.dma_start(out=out_groups[side][g], in_=probs[:])
+            soft[n, pair] = (probs, total)
+
+        def normalise_and_store(n, pair):
+            g, side = divmod(n, SIDES)
+            probs, total = soft[n, pair]
+            inverse = stat_pool.tile([P, 2], F32)
+            nc.gpsimd.tensor_tensor(out=inverse[:], in0=total[:], in1=minus_one[:], op=ALU.pow)
+            for i in range(2):
+                nc.scalar.activation(
+                    out=probs[:, i, :],
+                    in_=probs[:, i, :],
+                    func=ACT.Copy,
+                    scale=inverse[:, i : i + 1],
+                )
+            nc.sync.dma_start(
+                out=out_groups[side][g][:, 2 * pair : 2 * pair + 2, :], in_=probs[:]
+            )
 
         for h in range(3):
             transpose_x(h)
@@ -255,13 +256,15 @@ def tile_slotmemoryphasor_pa_t_kernel(
         for n in range(UNITS + 2):
             if n < UNITS:
                 project(n)
+            if n + 3 < HALVES:
+                transpose_x(n + 3)
             if n >= 2:
-                normalise_and_store(n - 2)
+                for pair in range(PAIRS):
+                    normalise_and_store(n - 2, pair)
             if n + 2 < HALVES:
                 quantise_x(n + 2)
             if 1 <= n <= UNITS:
-                score(n - 1)
-            if n + 3 < HALVES:
-                transpose_x(n + 3)
+                for pair in range(PAIRS):
+                    score(n - 1, pair)
             if n < UNITS:
                 quantise_kq(n)

@@ -50,16 +50,13 @@ def tile_slotmemoryphasor_pa_t_kernel(
         psum_s = ctx.enter_context(tc.psum_pool(name="psum_s", bufs=2))
 
         w_raw = {}
-        for side, w in enumerate((Wk, Wq)):
-            w_rows = w.rearrange("(c u p e) n -> c p u e n", c=D_PASSES, u=2, p=P, e=2)
-            for c in range(D_PASSES):
-                w_raw[side, c] = const.tile([P, PACK, D_KEY], BF16, name="w_raw%d%d" % (side, c))
-                nc.sync.dma_start(
-                    out=w_raw[side, c][:].rearrange("p (u e) n -> p u e n", u=2),
-                    in_=w_rows[c],
-                )
-        sk_sb = const.tile([P, SLOTS // P, D_KEY], BF16)
-        nc.sync.dma_start(out=sk_sb[:], in_=slot_keys.rearrange("(blk p) e -> p blk e", p=P))
+
+        def load_w(side, c):
+            w_rows = (Wk, Wq)[side].rearrange("(c u p e) n -> c p u e n", c=D_PASSES, u=2, p=P, e=2)
+            w_raw[side, c] = const.tile([P, PACK, D_KEY], BF16, name="w_raw%d%d" % (side, c))
+            nc.sync.dma_start(
+                out=w_raw[side, c][:].rearrange("p (u e) n -> p u e n", u=2), in_=w_rows[c]
+            )
 
         x_halves = x.flatten_outer_dims().rearrange(
             "(g p j) (c d) -> g c p j d", p=P, j=TILES, c=D_PASSES
@@ -69,9 +66,21 @@ def tile_slotmemoryphasor_pa_t_kernel(
             for o in (out_0, out_1)
         ]
         x_sb = []
-        for h in range(HALVES):
+
+        def load_x(h):
             x_sb.append(x_pool.tile([P, TILES, K_PASS], BF16, name="x_sb%d" % h))
             nc.sync.dma_start(out=x_sb[h][:], in_=x_halves[h // D_PASSES, h % D_PASSES])
+
+        load_w(0, 0)
+        load_x(0)
+        load_w(0, 1)
+        load_x(1)
+        load_w(1, 0)
+        load_w(1, 1)
+        sk_sb = const.tile([P, SLOTS // P, D_KEY], BF16)
+        nc.sync.dma_start(out=sk_sb[:], in_=slot_keys.rearrange("(blk p) e -> p blk e", p=P))
+        for h in range(2, HALVES):
+            load_x(h)
 
         scale_bf = const.tile([P, 1], BF16)
         nc.scalar.dma_start(out=scale_bf[:], in_=scale.partition_broadcast(P))
@@ -95,42 +104,22 @@ def tile_slotmemoryphasor_pa_t_kernel(
         w_codes = const.tile([P, SIDES, D_PASSES, D_KEY], U32, align_bytes=64)
         w_scales = const.tile([P, SIDES, D_PASSES, D_KEY], U8, align_bytes=64)
         w_grouped = {}
-        for side in range(SIDES):
-            for c in range(D_PASSES):
-                w_grouped[side, c] = const.tile(
-                    [P, D_KEY * PACK], BF16, align_bytes=64, name="w_grouped%d%d" % (side, c)
-                )
-                nc.vector.tensor_copy(
-                    out=w_grouped[side, c][:].rearrange("p (m r t) -> p m r t", m=PACK, t=PACK),
-                    in_=w_raw[side, c][:].rearrange("p t (r m) -> p m r t", m=PACK),
-                )
-        for side in range(SIDES):
-            for c in range(D_PASSES):
-                nc.vector.quantize_mx(
-                    out=w_codes[:, side, c, :].bitcast(FP8X4),
-                    scales=w_scales[:, side, c, :],
-                    in_=w_grouped[side, c][:],
-                )
 
-        sk_t = psum_t.tile([P, 2, SLOTS], F32, tag="xt")
-        for blk in range(SLOTS // P):
-            sk_words = sk_sb[:, blk, :].bitcast(F32).rearrange("p (w u) -> p u w", u=2)
-            for u in range(2):
-                nc.tensor.transpose(
-                    sk_t[:, u, blk * P : (blk + 1) * P], sk_words[:, u, :], ident[:]
-                )
-        sk_grouped = const.tile([P, SLOTS * PACK], BF16, align_bytes=64)
-        nc.scalar.activation(
-            out=sk_grouped[:].rearrange("p (s u e) -> p s u e", u=2, e=2),
-            in_=sk_t[:].bitcast(BF16).rearrange("p u (s e) -> p s u e", e=2),
-            func=ACT.Copy,
-            scale=sign_scale[:],
-        )
-        sk_codes = const.tile([P, SLOTS], U32, align_bytes=64)
-        sk_scales = const.tile([P, SLOTS], U8, align_bytes=64)
-        nc.vector.quantize_mx(
-            out=sk_codes[:].bitcast(FP8X4), scales=sk_scales[:], in_=sk_grouped[:]
-        )
+        def regroup_w(side, c, copy):
+            w_grouped[side, c] = const.tile(
+                [P, D_KEY * PACK], BF16, align_bytes=64, name="w_grouped%d%d" % (side, c)
+            )
+            copy(
+                out=w_grouped[side, c][:].rearrange("p (m r t) -> p m r t", m=PACK, t=PACK),
+                in_=w_raw[side, c][:].rearrange("p t (r m) -> p m r t", m=PACK),
+            )
+
+        def quantise_w(side, c):
+            nc.vector.quantize_mx(
+                out=w_codes[:, side, c, :].bitcast(FP8X4),
+                scales=w_scales[:, side, c, :],
+                in_=w_grouped[side, c][:],
+            )
 
         x_grouped = {}
         x_mx = {}
@@ -171,7 +160,7 @@ def tile_slotmemoryphasor_pa_t_kernel(
             )
             for j in range(TILES):
                 tokens = slice(j * P, (j + 1) * P)
-                acc = psum_p.tile([P, PACK, P], F32)
+                acc = psum_p.tile([P, PACK, P], F32, tag="acc", name="acc")
                 for m in range(PACK):
                     chunk = slice(m * P, (m + 1) * P)
                     for c in range(D_PASSES):
@@ -202,9 +191,12 @@ def tile_slotmemoryphasor_pa_t_kernel(
             )
             kq_mx[n] = (codes, scales)
 
-        def score(n, pair):
+        def score(n, pair, tail=False):
             codes, scales = kq_mx[n]
-            sc = psum_s.tile([P, 2, SLOTS], F32)
+            if tail:
+                sc = psum_p.tile([P, 2, SLOTS], F32, tag="acc", name="sc_tail")
+            else:
+                sc = psum_s.tile([P, 2, SLOTS], F32, name="sc")
             for i in range(2):
                 tokens = slice((2 * pair + i) * P, (2 * pair + i + 1) * P)
                 nc.tensor.matmul_mx(
@@ -219,7 +211,10 @@ def tile_slotmemoryphasor_pa_t_kernel(
             top = stat_pool.tile([P, 2], F32)
             nc.vector.tensor_reduce(out=top[:], in_=sc[:], axis=mybir.AxisListType.X, op=ALU.max)
             shift = stat_pool.tile([P, 2], F32)
-            nc.gpsimd.tensor_scalar_mul(out=shift[:], in0=top[:], scalar1=neg_abs_scale[:])
+            if tail:
+                nc.vector.tensor_scalar_mul(out=shift[:], in0=top[:], scalar1=neg_abs_scale[:])
+            else:
+                nc.gpsimd.tensor_scalar_mul(out=shift[:], in0=top[:], scalar1=neg_abs_scale[:])
             probs = out_pool.tile([P, 2, SLOTS], F32)
             total = stat_pool.tile([P, 2], F32)
             for i in range(2):
@@ -233,29 +228,69 @@ def tile_slotmemoryphasor_pa_t_kernel(
                 )
             soft[n, pair] = (probs, total)
 
-        def normalise_and_store(n, pair):
+        def normalise_and_store(n, pair, tail=False):
             g, side = divmod(n, SIDES)
             probs, total = soft[n, pair]
             inverse = stat_pool.tile([P, 2], F32)
-            nc.gpsimd.tensor_tensor(out=inverse[:], in0=total[:], in1=minus_one[:], op=ALU.pow)
+            if tail:
+                nc.vector.reciprocal(out=inverse[:], in_=total[:])
+            else:
+                nc.gpsimd.tensor_tensor(out=inverse[:], in0=total[:], in1=minus_one[:], op=ALU.pow)
             for i in range(2):
-                nc.scalar.activation(
-                    out=probs[:, i, :],
-                    in_=probs[:, i, :],
-                    func=ACT.Copy,
-                    scale=inverse[:, i : i + 1],
-                )
+                if tail and (i == 0 or n < UNITS - 1):
+                    nc.vector.tensor_scalar_mul(
+                        out=probs[:, i, :], in0=probs[:, i, :], scalar1=inverse[:, i : i + 1]
+                    )
+                else:
+                    nc.scalar.activation(
+                        out=probs[:, i, :],
+                        in_=probs[:, i, :],
+                        func=ACT.Copy,
+                        scale=inverse[:, i : i + 1],
+                    )
             nc.sync.dma_start(
                 out=out_groups[side][g][:, 2 * pair : 2 * pair + 2, :], in_=probs[:]
             )
 
-        for h in range(3):
-            transpose_x(h)
-        for h in range(2):
-            quantise_x(h)
-        for n in range(UNITS + 2):
-            if n < UNITS:
-                project(n)
+        def prepare_slot_keys():
+            sk_t = psum_t.tile([P, 2, SLOTS], F32, tag="xt")
+            for blk in range(SLOTS // P):
+                sk_words = sk_sb[:, blk, :].bitcast(F32).rearrange("p (w u) -> p u w", u=2)
+                for u in range(2):
+                    nc.tensor.transpose(
+                        sk_t[:, u, blk * P : (blk + 1) * P], sk_words[:, u, :], ident[:]
+                    )
+            sk_grouped = const.tile([P, SLOTS * PACK], BF16, align_bytes=64)
+            nc.scalar.activation(
+                out=sk_grouped[:].rearrange("p (s u e) -> p s u e", u=2, e=2),
+                in_=sk_t[:].bitcast(BF16).rearrange("p u (s e) -> p s u e", e=2),
+                func=ACT.Copy,
+                scale=sign_scale[:],
+            )
+            sk_codes = const.tile([P, SLOTS], U32, align_bytes=64)
+            sk_scales = const.tile([P, SLOTS], U8, align_bytes=64)
+            nc.vector.quantize_mx(
+                out=sk_codes[:].bitcast(FP8X4), scales=sk_scales[:], in_=sk_grouped[:]
+            )
+            return sk_codes, sk_scales
+
+        regroup_w(0, 0, nc.vector.tensor_copy)
+        transpose_x(0)
+        quantise_w(0, 0)
+        transpose_x(1)
+        regroup_w(0, 1, nc.vector.tensor_copy)
+        quantise_w(0, 1)
+        quantise_x(0)
+        quantise_x(1)
+        regroup_w(1, 0, nc.scalar.copy)
+        regroup_w(1, 1, nc.vector.tensor_copy)
+        for n in range(UNITS):
+            project(n)
+            if n == 0:
+                quantise_w(1, 0)
+                quantise_w(1, 1)
+                sk_codes, sk_scales = prepare_slot_keys()
+                transpose_x(2)
             if n + 3 < HALVES:
                 transpose_x(n + 3)
             if n >= 2:
@@ -263,8 +298,15 @@ def tile_slotmemoryphasor_pa_t_kernel(
                     normalise_and_store(n - 2, pair)
             if n + 2 < HALVES:
                 quantise_x(n + 2)
-            if 1 <= n <= UNITS:
+            if n == UNITS - 1:
+                quantise_kq(n)
+            if n >= 1:
                 for pair in range(PAIRS):
                     score(n - 1, pair)
-            if n < UNITS:
+            if n < UNITS - 1:
                 quantise_kq(n)
+        for pair in range(PAIRS):
+            score(UNITS - 1, pair, tail=True)
+        for n in (UNITS - 2, UNITS - 1):
+            for pair in range(PAIRS):
+                normalise_and_store(n, pair, tail=True)

@@ -82,22 +82,23 @@ def tile_slotmemoryphasor_pa_t_kernel(
         for h in range(2, HALVES):
             load_x(h)
 
-        scale_bf = const.tile([P, 1], BF16)
-        nc.scalar.dma_start(out=scale_bf[:], in_=scale.partition_broadcast(P))
-        bias = []
+        vectors = const.tile([P, SIDES * D_KEY + 2], BF16)
+        nc.vector.memset(vectors[:], 0.0)
+        ones = const.tile([P, P], BF16)
+        nc.vector.memset(ones[:], 1.0)
         for side, b in enumerate((bk, bq)):
-            bias.append(const.tile([P, PACK], BF16, name="bias%d" % side))
-            nc.scalar.dma_start(out=bias[side][:], in_=b.rearrange("(p m) -> p m", m=PACK))
+            nc.scalar.dma_start(
+                out=vectors[0:1, side * D_KEY : (side + 1) * D_KEY],
+                in_=b.rearrange("(o n) -> o n", o=1),
+            )
+        nc.scalar.dma_start(
+            out=vectors[0:1, SIDES * D_KEY : SIDES * D_KEY + 1],
+            in_=scale.rearrange("(o n) -> o n", o=1),
+        )
 
         ident = const.tile([P, P], F32)
         make_identity(nc, ident[:])
 
-        sign_scale = const.tile([P, 1], F32)
-        nc.scalar.activation(out=sign_scale[:], in_=scale_bf[:], func=ACT.Sign)
-        abs_scale = const.tile([P, 1], F32)
-        nc.scalar.activation(out=abs_scale[:], in_=scale_bf[:], func=ACT.Abs)
-        neg_abs_scale = const.tile([P, 1], F32)
-        nc.scalar.mul(out=neg_abs_scale[:], in_=abs_scale[:], mul=-1.0)
         minus_one = const.tile([P, 2], F32)
         nc.gpsimd.memset(minus_one[:], -1.0)
 
@@ -153,6 +154,10 @@ def tile_slotmemoryphasor_pa_t_kernel(
             )
             x_mx[h] = (codes, scales)
 
+        small = const.tile([P, SIDES * PACK + 1], F32)
+        bias = [small[:, side * PACK : (side + 1) * PACK] for side in range(SIDES)]
+        scale_all = small[:, SIDES * PACK : SIDES * PACK + 1]
+
         def project(n):
             g, side = divmod(n, SIDES)
             kq_grouped[n] = kq_pool.tile(
@@ -179,7 +184,7 @@ def tile_slotmemoryphasor_pa_t_kernel(
                         "p (r m) -> p r m", m=PACK
                     ),
                     in0=acc[:].rearrange("p m r -> p r m"),
-                    in1=bias[side][:].unsqueeze(1).to_broadcast([P, P, PACK]),
+                    in1=bias[side].unsqueeze(1).to_broadcast([P, P, PACK]),
                     op=ALU.add,
                 )
 
@@ -282,6 +287,32 @@ def tile_slotmemoryphasor_pa_t_kernel(
         quantise_w(0, 1)
         quantise_x(0)
         quantise_x(1)
+        spread = psum_t.tile([P, SIDES * PACK + 1], F32, tag="xt", name="spread")
+        for side in range(SIDES):
+            for m in range(PACK):
+                k = side * PACK + m
+                nc.tensor.matmul(
+                    out=spread[:, k : k + 1],
+                    lhsT=vectors[:, side * D_KEY + m : (side + 1) * D_KEY : PACK],
+                    rhs=ones[:, 0:1],
+                    start=True,
+                    stop=True,
+                )
+        nc.tensor.matmul(
+            out=spread[:, SIDES * PACK : SIDES * PACK + 1],
+            lhsT=ones[:],
+            rhs=vectors[:, SIDES * D_KEY : SIDES * D_KEY + 1],
+            start=True,
+            stop=True,
+        )
+        nc.scalar.copy(out=small[:], in_=spread[:])
+
+        sign_scale = const.tile([P, 1], F32)
+        nc.scalar.activation(out=sign_scale[:], in_=scale_all, func=ACT.Sign)
+        abs_scale = const.tile([P, 1], F32)
+        nc.scalar.activation(out=abs_scale[:], in_=scale_all, func=ACT.Abs)
+        neg_abs_scale = const.tile([P, 1], F32)
+        nc.scalar.mul(out=neg_abs_scale[:], in_=abs_scale[:], mul=-1.0)
         regroup_w(1, 0, nc.scalar.copy)
         regroup_w(1, 1, nc.vector.tensor_copy)
         for n in range(UNITS):

from contextlib import ExitStack

import concourse.mybir as mybir
from concourse.masks import make_identity

F32 = mybir.dt.float32
BF16 = mybir.dt.bfloat16
U32 = mybir.dt.uint32
U8 = mybir.dt.uint8
FP8X4 = mybir.dt.float8_e4m3fn_x4
ACT = mybir.ActivationFunctionType
ALU = mybir.AluOpType

P = 128
PACK = 4
K_PASS = P * PACK

TOKENS = 4096
D_MODEL = 1024
D_KEY = 512
SLOTS = 256
D_PASSES = D_MODEL // K_PASS

GROUP = 512
TILES = GROUP // P
GROUPS = TOKENS // GROUP
SIDES = 2
HALVES = GROUPS * D_PASSES
UNITS = GROUPS * SIDES
PAIRS = TILES // 2

FLOPS = 2 * TOKENS * D_MODEL * SIDES * D_KEY + 2 * TOKENS * D_KEY * SIDES * SLOTS


def tile_slotmemoryphasor_pa_t_kernel(
    tc, x, Wk, bk, Wq, bq, slot_keys, scale, out_0, out_1
):
    nc = tc.nc
    with ExitStack() as ctx:
        ctx.enter_context(tc.manual_schedule())
        const = ctx.enter_context(tc.tile_pool(name="const", bufs=1))
        x_pool = ctx.enter_context(tc.tile_pool(name="x_pool", bufs=1))
        xg_pool = ctx.enter_context(tc.tile_pool(name="xg_pool", bufs=3))
        xq_pool = ctx.enter_context(tc.tile_pool(name="xq_pool", bufs=4))
        kq_pool = ctx.enter_context(tc.tile_pool(name="kq_pool", bufs=2))
        out_pool = ctx.enter_context(tc.tile_pool(name="out_pool", bufs=8))
        stat_pool = ctx.enter_context(tc.tile_pool(name="stat_pool", bufs=8))
        psum_t = ctx.enter_context(tc.psum_pool(name="psum_t", bufs=2))
        psum_p = ctx.enter_context(tc.psum_pool(name="psum_p", bufs=4))
        psum_s = ctx.enter_context(tc.psum_pool(name="psum_s", bufs=2))

        w_raw = {}

        def load_w(side, c):
            w_rows = (Wk, Wq)[side].rearrange("(c u p e) n -> c p u e n", c=D_PASSES, u=2, p=P, e=2)
            w_raw[side, c] = const.tile([P, PACK, D_KEY], BF16, name="w_raw%d%d" % (side, c))
            nc.sync.dma_start(
                out=w_raw[side, c][:].rearrange("p (u e) n -> p u e n", u=2), in_=w_rows[c]
            )

        x_halves = x.flatten_outer_dims().rearrange(
            "(g p j) (c d) -> g c p j d", p=P, j=TILES, c=D_PASSES
        )
        out_groups = [
            o.flatten_outer_dims().rearrange("(g p j) s -> g p j s", p=P, j=TILES)
            for o in (out_0, out_1)
        ]
        x_sb = []

        def load_x(h):
            x_sb.append(x_pool.tile([P, TILES, K_PASS], BF16, name="x_sb%d" % h))
            nc.sync.dma_start(out=x_sb[h][:], in_=x_halves[h // D_PASSES, h % D_PASSES])

        load_w(0, 0)
        load_x(0)
        load_w(0, 1)
        load_x(1)
        load_w(1, 0)
        load_w(1, 1)
        sk_sb = const.tile([P, SLOTS // P, D_KEY], BF16)
        nc.sync.dma_start(out=sk_sb[:], in_=slot_keys.rearrange("(blk p) e -> p blk e", p=P))
        for h in range(2, HALVES):
            load_x(h)

        vectors = const.tile([P, SIDES * D_KEY + 2], BF16)
        nc.vector.memset(vectors[:], 0.0)
        ones = const.tile([P, P], BF16)
        nc.vector.memset(ones[:], 1.0)
        for side, b in enumerate((bk, bq)):
            nc.scalar.dma_start(
                out=vectors[0:1, side * D_KEY : (side + 1) * D_KEY],
                in_=b.rearrange("(o n) -> o n", o=1),
            )
        nc.scalar.dma_start(
            out=vectors[0:1, SIDES * D_KEY : SIDES * D_KEY + 1],
            in_=scale.rearrange("(o n) -> o n", o=1),
        )

        ident = const.tile([P, P], F32)
        make_identity(nc, ident[:])

        minus_one = const.tile([P, 2], F32)
        nc.gpsimd.memset(minus_one[:], -1.0)

        w_codes = const.tile([P, SIDES, D_PASSES, D_KEY], U32, align_bytes=64)
        w_scales = const.tile([P, SIDES, D_PASSES, D_KEY], U8, align_bytes=64)
        w_grouped = {}

        def regroup_w(side, c, copy):
            w_grouped[side, c] = const.tile(
                [P, D_KEY * PACK], BF16, align_bytes=64, name="w_grouped%d%d" % (side, c)
            )
            copy(
                out=w_grouped[side, c][:].rearrange("p (m r t) -> p m r t", m=PACK, t=PACK),
                in_=w_raw[side, c][:].rearrange("p t (r m) -> p m r t", m=PACK),
            )

        def quantise_w(side, c):
            nc.vector.quantize_mx(
                out=w_codes[:, side, c, :].bitcast(FP8X4),
                scales=w_scales[:, side, c, :],
                in_=w_grouped[side, c][:],
            )

        x_grouped = {}
        x_mx = {}
        kq_grouped = {}
        kq_mx = {}
        soft = {}

        def transpose_x(h):
            x_grouped[h] = xg_pool.tile([P, GROUP * PACK], BF16, align_bytes=64, name="x_grouped")
            for pair in range(PAIRS):
                xt = psum_t.tile([P, 2, 2 * P], F32, tag="xt")
                for u in range(2):
                    for i in range(2):
                        x_words = x_sb[h][:, 2 * pair + i, :].bitcast(F32)
                        nc.tensor.transpose(
                            xt[:, u, i * P : (i + 1) * P], x_words[:, u * P : (u + 1) * P], ident[:]
                        )
                width = GROUP * PACK // 2
                nc.scalar.copy(
                    out=x_grouped[h][:, pair * width : (pair + 1) * width]
                    .bitcast(F32)
                    .rearrange("p (r u) -> p r u", u=2),
                    in_=xt[:].rearrange("p u r -> p r u"),
                )

        def quantise_x(h):
            codes = xq_pool.tile([P, GROUP], U32, align_bytes=64, name="x_codes")
            scales = xq_pool.tile([P, GROUP], U8, align_bytes=64, name="x_scales")
            nc.vector.quantize_mx(
                out=codes[:].bitcast(FP8X4), scales=scales[:], in_=x_grouped[h][:]
            )
            x_mx[h] = (codes, scales)

        small = const.tile([P, SIDES * PACK + 1], F32)
        bias = [small[:, side * PACK : (side + 1) * PACK] for side in range(SIDES)]
        scale_all = small[:, SIDES * PACK : SIDES * PACK + 1]

        def project(n):
            g, side = divmod(n, SIDES)
            kq_grouped[n] = kq_pool.tile(
                [P, GROUP * PACK], BF16, align_bytes=64, name="kq_grouped"
            )
            for j in range(TILES):
                tokens = slice(j * P, (j + 1) * P)
                acc = psum_p.tile([P, PACK, P], F32, tag="acc", name="acc")
                for m in range(PACK):
                    chunk = slice(m * P, (m + 1) * P)
                    for c in range(D_PASSES):
                        codes, scales = x_mx[D_PASSES * g + c]
                        nc.tensor.matmul_mx(
                            out=acc[:, m, :],
                            lhsT=w_codes[:, side, c, chunk].bitcast(FP8X4),
                            lhsT_scale=w_scales[:, side, c, chunk],
                            rhs=codes[:, tokens].bitcast(FP8X4),
                            rhs_scale=scales[:, tokens],
                            start=(c == 0),
                            stop=(c == D_PASSES - 1),
                        )
                nc.vector.tensor_tensor(
                    out=kq_grouped[n][:, j * K_PASS : (j + 1) * K_PASS].rearrange(
                        "p (r m) -> p r m", m=PACK
                    ),
                    in0=acc[:].rearrange("p m r -> p r m"),
                    in1=bias[side].unsqueeze(1).to_broadcast([P, P, PACK]),
                    op=ALU.add,
                )

        def quantise_kq(n):
            codes = kq_pool.tile([P, GROUP], U32, align_bytes=64, name="kq_codes")
            scales = kq_pool.tile([P, GROUP], U8, align_bytes=64, name="kq_scales")
            nc.vector.quantize_mx(
                out=codes[:].bitcast(FP8X4), scales=scales[:], in_=kq_grouped[n][:]
            )
            kq_mx[n] = (codes, scales)

        def score(n, pair, tail=False):
            codes, scales = kq_mx[n]
            if tail:
                sc = psum_p.tile([P, 2, SLOTS], F32, tag="acc", name="sc_tail")
            else:
                sc = psum_s.tile([P, 2, SLOTS], F32, name="sc")
            for i in range(2):
                tokens = slice((2 * pair + i) * P, (2 * pair + i + 1) * P)
                nc.tensor.matmul_mx(
                    out=sc[:, i, :],
                    lhsT=codes[:, tokens].bitcast(FP8X4),
                    lhsT_scale=scales[:, tokens],
                    rhs=sk_codes[:].bitcast(FP8X4),
                    rhs_scale=sk_scales[:],
                    start=True,
                    stop=True,
                )
            top = stat_pool.tile([P, 2], F32)
            nc.vector.tensor_reduce(out=top[:], in_=sc[:], axis=mybir.AxisListType.X, op=ALU.max)
            shift = stat_pool.tile([P, 2], F32)
            if tail:
                nc.vector.tensor_scalar_mul(out=shift[:], in0=top[:], scalar1=neg_abs_scale[:])
            else:
                nc.gpsimd.tensor_scalar_mul(out=shift[:], in0=top[:], scalar1=neg_abs_scale[:])
            probs = out_pool.tile([P, 2, SLOTS], F32)
            total = stat_pool.tile([P, 2], F32)
            for i in range(2):
                nc.scalar.activation(
                    out=probs[:, i, :],
                    in_=sc[:, i, :],
                    func=ACT.Exp,
                    bias=shift[:, i : i + 1],
                    scale=abs_scale[:],
                    accum_out=total[:, i : i + 1],
                )
            soft[n, pair] = (probs, total)

        def normalise_and_store(n, pair, tail=False):
            g, side = divmod(n, SIDES)
            probs, total = soft[n, pair]
            inverse = stat_pool.tile([P, 2], F32)
            if tail:
                nc.vector.reciprocal(out=inverse[:], in_=total[:])
            else:
                nc.gpsimd.tensor_tensor(out=inverse[:], in0=total[:], in1=minus_one[:], op=ALU.pow)
            for i in range(2):
                if tail and (i == 0 or n < UNITS - 1):
                    nc.vector.tensor_scalar_mul(
                        out=probs[:, i, :], in0=probs[:, i, :], scalar1=inverse[:, i : i + 1]
                    )
                else:
                    nc.scalar.activation(
                        out=probs[:, i, :],
                        in_=probs[:, i, :],
                        func=ACT.Copy,
                        scale=inverse[:, i : i + 1],
                    )
            nc.sync.dma_start(
                out=out_groups[side][g][:, 2 * pair : 2 * pair + 2, :], in_=probs[:]
            )

        def prepare_slot_keys():
            sk_t = psum_t.tile([P, 2, SLOTS], F32, tag="xt")
            for blk in range(SLOTS // P):
                sk_words = sk_sb[:, blk, :].bitcast(F32).rearrange("p (w u) -> p u w", u=2)
                for u in range(2):
                    nc.tensor.transpose(
                        sk_t[:, u, blk * P : (blk + 1) * P], sk_words[:, u, :], ident[:]
                    )
            sk_grouped = const.tile([P, SLOTS * PACK], BF16, align_bytes=64)
            nc.scalar.activation(
                out=sk_grouped[:].rearrange("p (s u e) -> p s u e", u=2, e=2),
                in_=sk_t[:].bitcast(BF16).rearrange("p u (s e) -> p s u e", e=2),
                func=ACT.Copy,
                scale=sign_scale[:],
            )
            sk_codes = const.tile([P, SLOTS], U32, align_bytes=64)
            sk_scales = const.tile([P, SLOTS], U8, align_bytes=64)
            nc.vector.quantize_mx(
                out=sk_codes[:].bitcast(FP8X4), scales=sk_scales[:], in_=sk_grouped[:]
            )
            return sk_codes, sk_scales

        regroup_w(0, 0, nc.vector.tensor_copy)
        transpose_x(0)
        quantise_w(0, 0)
        transpose_x(1)
        regroup_w(0, 1, nc.vector.tensor_copy)
        quantise_w(0, 1)
        quantise_x(0)
        quantise_x(1)
        spread = psum_t.tile([P, SIDES * PACK + 1], F32, tag="xt", name="spread")
        for side in range(SIDES):
            for m in range(PACK):
                k = side * PACK + m
                nc.tensor.matmul(
                    out=spread[:, k : k + 1],
                    lhsT=vectors[:, side * D_KEY + m : (side + 1) * D_KEY : PACK],
                    rhs=ones[:, 0:1],
                    start=True,
                    stop=True,
                )
        nc.tensor.matmul(
            out=spread[:, SIDES * PACK : SIDES * PACK + 1],
            lhsT=ones[:],
            rhs=vectors[:, SIDES * D_KEY : SIDES * D_KEY + 1],
            start=True,
            stop=True,
        )
        nc.scalar.copy(out=small[:], in_=spread[:])

        sign_scale = const.tile([P, 1], F32)
        nc.scalar.activation(out=sign_scale[:], in_=scale_all, func=ACT.Sign)
        abs_scale = const.tile([P, 1], F32)
        nc.scalar.activation(out=abs_scale[:], in_=scale_all, func=ACT.Abs)
        neg_abs_scale = const.tile([P, 1], F32)
        nc.scalar.mul(out=neg_abs_scale[:], in_=abs_scale[:], mul=-1.0)
        regroup_w(1, 0, nc.scalar.copy)
        regroup_w(1, 1, nc.vector.tensor_copy)
        for n in range(UNITS):
            project(n)
            if n == 0:
                quantise_w(1, 0)
                quantise_w(1, 1)
                sk_codes, sk_scales = prepare_slot_keys()
                transpose_x(2)
            if n + 3 < HALVES:
                transpose_x(n + 3)
            if n >= 2:
                for pair in range(PAIRS):
                    normalise_and_store(n - 2, pair)
            if n + 2 < HALVES:
                quantise_x(n + 2)
            if n == UNITS - 1:
                quantise_kq(n)
            if n >= 1:
                for pair in range(PAIRS):
                    score(n - 1, pair)
            if n < UNITS - 1:
                quantise_kq(n)
        for pair in range(PAIRS):
            score(UNITS - 1, pair, tail=True)
        for n in (UNITS - 2, UNITS - 1):
            for pair in range(PAIRS):
                normalise_and_store(n, pair, tail=True)
